import numpy as np
import ml_dtypes


def mxq(x, axis, fmt="e4m3"):
    dtype, down = {"e4m3": (ml_dtypes.float8_e4m3fn, 7), "e5m2": (ml_dtypes.float8_e5m2, 14)}[fmt]
    v = np.moveaxis(np.asarray(x, np.float32).astype(ml_dtypes.bfloat16).astype(np.float64), axis, -1)
    blocks = v.reshape(v.shape[:-1] + (-1, 32))
    amax = np.abs(blocks).max(-1, keepdims=True)
    byte = np.maximum(np.where(amax > 0, np.frexp(amax)[1] - 1 + 127, 0) - down, 1)
    scale = np.exp2(byte - 127.0)
    codes = (blocks / scale).astype(np.float32).astype(dtype).astype(np.float64)
    return np.moveaxis((codes * scale).reshape(v.shape), -1, axis)


WIDE = False


def mx_kscale(k):
    if not WIDE:
        return np.ones(k)
    levels = np.array([10, -10, 5, -5, 0])
    a = np.random.permutation(np.resize(levels, k // 512 * 4)).reshape(k // 512, 4)
    idx = np.arange(k)
    return np.exp2(a[idx // 512, idx % 128 // 32])


BF16 = ml_dtypes.bfloat16


def bf(x):
    return np.asarray(x, np.float32).astype(BF16)


def f64(x):
    return np.asarray(x).astype(np.float64)


B, L, C, K = 512, 8, 512, 5
F = C
BN_EPS = 1e-3
LEAKY_ALPHA = 0.3


def leaky(v):
    return np.where(v >= 0, v, LEAKY_ALPHA * v)


def bn(v, gamma, beta, mean, var):
    return gamma * (v - mean) * (1.0 / np.sqrt(var + BN_EPS)) + beta


def setup_inputs():
    s = mx_kscale(F)
    return {"h": bf(leaky(np.random.standard_normal((B, L, F)) * 1.2) * s),
            "x": bf(np.random.standard_normal((B, L, C))),
            "k2": bf(np.random.standard_normal((K, L, F, F)) * 0.16 / np.sqrt(K * F) / s[:, None]),
            "b2": bf(np.random.standard_normal((L, F)) * 0.03),
            "gamma2": bf(1.0 + 0.1 * np.random.standard_normal(F)),
            "beta2": bf(np.random.standard_normal(F) * 0.2),
            "mean2": bf(np.random.standard_normal(F) * 0.05),
            "var2": bf(np.random.uniform(0.01, 0.03, F))}


def reference(h, x, k2, b2, gamma2, beta2, mean2, var2):
    hq = mxq(f64(h).transpose(1, 0, 2), 2, "e4m3")
    k = f64(k2)
    out = 2.0 * f64(b2)
    for i in range(k.shape[0]):
        step = (i // 2) * (-1 if i % 2 == 1 else 1)
        ki = np.roll(k[i], -step, axis=0) if step != 0 else k[i]
        p = hq @ mxq(ki, 1, "e4m3")
        p = np.roll(p, step, axis=0) if step != 0 else p
        out = out + p.transpose(1, 0, 2)
    return leaky(bn(out, f64(gamma2), f64(beta2), f64(mean2), f64(var2)) + f64(x))

@@ -1,0 +1,255 @@
+from contextlib import ExitStack
+
+import concourse.mybir as mybir
+from concourse.masks import make_identity
+
+FLOPS = 2 * 5 * 8 * 512 * 512 * 512
+
+F32 = mybir.dt.float32
+BF16 = mybir.dt.bfloat16
+U32 = mybir.dt.uint32
+U8 = mybir.dt.uint8
+FP8X4 = mybir.dt.float8_e4m3fn_x4
+ALU = mybir.AluOpType
+ACT = mybir.ActivationFunctionType
+
+P = 128
+L = 8
+TAPS = 5
+STEP = (0, 0, 1, -1, 2)
+BN_EPS = 1e-3
+ALPHA = 0.3
+N_CHUNKS = TAPS * L
+N_PAIRS = N_CHUNKS // 2
+RAW_BUFS = 6
+V_COLS = 192
+PIN = True
+
+
+def tile_residualblock5_pb_t_kernel(tc, h, x, k2, b2, gamma2, beta2, mean2, var2, out):
+    nc = tc.nc
+    with ExitStack() as ctx:
+        const = ctx.enter_context(tc.tile_pool(name="const", bufs=1))
+        rawp = ctx.enter_context(tc.tile_pool(name="rawp", bufs=RAW_BUFS))
+        grpp = ctx.enter_context(tc.tile_pool(name="grpp", bufs=4))
+        kwp = ctx.enter_context(tc.tile_pool(name="kwp", bufs=8))
+        sp = ctx.enter_context(tc.tile_pool(name="sp", bufs=8))
+        zpool = ctx.enter_context(tc.tile_pool(name="zpool", bufs=3))
+        ps_a = ctx.enter_context(tc.psum_pool(name="ps_a", bufs=4))
+        ps_b = ctx.enter_context(tc.psum_pool(name="ps_b", bufs=4))
+        if PIN:
+            ctx.enter_context(tc.manual_schedule())
+
+        ident_f = const.tile([P, P], F32, name="ident_f")
+        make_identity(nc, ident_f[:])
+        ident_b = const.tile([P, P], BF16, name="ident_b")
+        warm = const.tile([P, 1], F32, name="warm")
+        nc.vector.memset(warm[:], 1.0)
+        cst = const.tile([P, P], BF16, name="cst")
+        nc.vector.memset(cst[:], 0.0)
+        nc.scalar.dma_start(out=cst[0:4, :], in_=gamma2.rearrange("(r c) -> r c", c=P))
+        nc.scalar.dma_start(out=cst[4:8, :], in_=beta2.rearrange("(r c) -> r c", c=P))
+        nc.scalar.dma_start(out=cst[8:12, :], in_=mean2.rearrange("(r c) -> r c", c=P))
+        nc.scalar.dma_start(out=cst[12:16, :], in_=var2.rearrange("(r c) -> r c", c=P))
+        nc.scalar.dma_start(out=cst[16:48, :], in_=b2.rearrange("l (r c) -> (l r) c", c=P))
+        nc.scalar.activation(out=warm[:], in_=warm[:], func=ACT.Sqrt)
+        nc.vector.tensor_copy(out=ident_b[:], in_=ident_f[:])
+
+        raws = {}
+        grps = {}
+        kws = {}
+        kss = {}
+
+        h_raw = []
+        for bt in range(4):
+            hr = rawp.tile([P, 4096], BF16, tag="raw", name="hraw")
+            nc.sync.dma_start(out=hr[:], in_=h[bt * P:(bt + 1) * P].rearrange("b l c -> b (l c)"))
+            h_raw.append(hr)
+
+        def load_pair(j):
+            rt = rawp.tile([P, 4096], BF16, tag="raw", name="kraw")
+            for hf in range(2):
+                li, i = divmod(2 * j + hf, TAPS)
+                nc.sync.dma_start(
+                    out=rt[:, hf * 2048:(hf + 1) * 2048],
+                    in_=k2[i, li].rearrange("(p t) f -> p (t f)", t=4),
+                )
+            raws[j] = rt
+
+        xs = {}
+
+        def load_x(half):
+            for bt in range(4):
+                xt = const.tile([P, 2048], BF16, name="x_%d_%d" % (bt, half))
+                nc.sync.dma_start(
+                    out=xt[:],
+                    in_=x[bt * P:(bt + 1) * P, half * 4:(half + 1) * 4, :].rearrange("b l f -> b (l f)"),
+                )
+                xs[(bt, half)] = xt
+
+        load_pair(0)
+        load_pair(1)
+
+        c_t = const.tile([P, 48], F32, name="c_t")
+        t_var = const.tile([P, 4], F32, name="t_var")
+        t_std = const.tile([P, 4], F32, name="t_std")
+        t_rstd = const.tile([P, 4], F32, name="t_rstd")
+        a_sc = const.tile([P, 4], F32, name="a_sc")
+        b_sc = const.tile([P, L, 4], F32, name="b_sc")
+
+        hg = []
+        hw = []
+        hs = []
+        for mp in range(4):
+            hg.append(grpp.tile([P, 4096], BF16, tag="grp", name="hgrp", align_bytes=64))
+            hw.append(const.tile([P, 1024], U32, name="hw%d" % mp, align_bytes=64))
+            hs.append(const.tile([P, 1024], U8, name="hs%d" % mp, align_bytes=64))
+
+        for bt in range(4):
+            hv = h_raw[bt][:].bitcast(F32).rearrange("b (m p u) -> b m u p", p=P, u=2)
+            for mp in range(4):
+                if mp % 2 == 0:
+                    tp = ps_a.tile([P, 2, 2, P], F32, tag="acc", name="tp_a")
+                else:
+                    tp = ps_b.tile([P, 2, 2, P], F32, tag="zp", name="tp_b")
+                for mi in range(2):
+                    for u in range(2):
+                        nc.tensor.transpose(tp[:, mi, u, :], hv[:, 2 * mp + mi, u, :], ident_f[:])
+                dst = hg[mp][:].bitcast(F32).rearrange("p (m b u) -> p m b u", m=2, u=2)[:, :, bt * P:(bt + 1) * P, :]
+                src = tp[:].rearrange("p m u b -> p m b u")
+                if mp % 2 == 0:
+                    nc.vector.tensor_copy(out=dst, in_=src)
+                else:
+                    nc.scalar.copy(out=dst, in_=src)
+            load_pair(2 + bt)
+            if bt == 0:
+                cps = ps_b.tile([P, P], BF16, tag="zp", name="cps")
+                nc.tensor.transpose(cps[:], cst[:], ident_b[:])
+                nc.vector.tensor_copy(out=c_t[:], in_=cps[:, 0:48])
+                nc.vector.tensor_scalar(out=t_var[:], in0=c_t[:, 12:16], scalar1=BN_EPS, scalar2=None, op0=ALU.add)
+            if bt == 1:
+                nc.scalar.activation(out=t_std[:], in_=t_var[:], func=ACT.Sqrt)
+            if bt == 2:
+                load_x(0)
+                nc.vector.reciprocal(out=t_rstd[:], in_=t_std[:])
+                nc.vector.tensor_tensor(out=a_sc[:], in0=t_rstd[:], in1=c_t[:, 0:4], op=ALU.mult)
+                nc.vector.scalar_tensor_tensor(
+                    out=b_sc[:],
+                    in0=c_t[:, 16:48].rearrange("p (l r) -> p l r", r=4),
+                    scalar=2.0,
+                    in1=c_t[:, 8:12].unsqueeze(1).to_broadcast([P, L, 4]),
+                    op0=ALU.mult,
+                    op1=ALU.subtract,
+                )
+                nc.vector.tensor_tensor(
+                    out=b_sc[:], in0=b_sc[:], in1=a_sc[:].unsqueeze(1).to_broadcast([P, L, 4]), op=ALU.mult
+                )
+                nc.vector.tensor_tensor(
+                    out=b_sc[:], in0=b_sc[:], in1=c_t[:, 4:8].unsqueeze(1).to_broadcast([P, L, 4]), op=ALU.add
+                )
+        for mp in range(4):
+            nc.vector.quantize_mx(out=hw[mp][:].bitcast(FP8X4), scales=hs[mp][:], in_=hg[mp][:])
+
+        def regroup(n):
+            j, hf = divmod(n, 2)
+            if hf == 0:
+                grps[j] = grpp.tile([P, 4096], BF16, tag="grp", name="kgrp", align_bytes=64)
+            src = raws[j][:, hf * 2048:(hf + 1) * 2048].rearrange("p (t c i) -> p c t i", t=4, i=4)
+            dst = grps[j][:, hf * 2048:(hf + 1) * 2048].rearrange("p (c i t) -> p c t i", i=4, t=4)
+            cv = V_COLS // 4
+            nc.vector.tensor_copy(out=dst[:, 0:cv], in_=src[:, 0:cv])
+            nc.scalar.copy(out=dst[:, cv:], in_=src[:, cv:])
+
+        def quantise(j):
+            kws[j] = kwp.tile([P, 1024], U32, tag="kw", name="kw", align_bytes=64)
+            kss[j] = kwp.tile([P, 1024], U8, tag="ks", name="ks", align_bytes=64)
+            nc.vector.quantize_mx(out=kws[j][:].bitcast(FP8X4), scales=kss[j][:], in_=grps[j][:])
+
+        def step(k):
+            if k < N_CHUNKS:
+                regroup(k)
+                if k % 2 == 1:
+                    j = (k - 1) // 2 + RAW_BUFS
+                    if j < N_PAIRS:
+                        load_pair(j)
+                    if j == 16:
+                        load_x(1)
+            if k >= 3 and k % 2 == 1 and (k - 3) // 2 < N_PAIRS:
+                quantise((k - 3) // 2)
+
+        accs = {}
+        s_tiles = {}
+
+        def mx_pass(li, ft, i):
+            m = (li - STEP[i]) % L
+            j, hf = divmod(TAPS * li + i, 2)
+            kc = slice(hf * 512 + ft * P, hf * 512 + (ft + 1) * P)
+            hc = slice((m % 2) * 512, (m % 2) * 512 + 512)
+            nc.tensor.matmul_mx(
+                out=accs[ft][:],
+                lhsT=kws[j][:, kc].bitcast(FP8X4),
+                lhsT_scale=kss[j][:, kc],
+                rhs=hw[m // 2][:, hc].bitcast(FP8X4),
+                rhs_scale=hs[m // 2][:, hc],
+                start=(i == 0),
+                stop=(i == TAPS - 1),
+            )
+
+        def new_acc(ft):
+            accs[ft] = ps_a.tile([P, 512], F32, tag="acc", name="acc")
+
+        def p1(li, ft):
+            st = sp.tile([P, 512], F32, tag="s", name="s")
+            nc.scalar.activation(
+                out=st[:], in_=accs[ft][:], func=ACT.Identity,
+                scale=a_sc[:, ft:ft + 1], bias=b_sc[:, li, ft:ft + 1],
+            )
+            s_tiles[(li, ft)] = st
+
+        out_v = out.rearrange("(t p) l f -> p t l f", p=P)
+
+        def back(li, fine):
+            z = zpool.tile([P, 4, 512], F32, tag="z", name="z")
+            for bt in range(4):
+                zp = ps_b.tile([P, 512], F32, tag="zp", name="zp")
+                for ft in range(4):
+                    nc.tensor.transpose(
+                        zp[:, ft * P:(ft + 1) * P], s_tiles[(li, ft)][:, bt * P:(bt + 1) * P], ident_f[:]
+                    )
+                xt = xs[(bt, li // 4)]
+                nc.vector.tensor_tensor(
+                    out=z[:, bt, :], in0=zp[:], in1=xt[:, (li % 4) * 512:(li % 4 + 1) * 512], op=ALU.add
+                )
+                if fine:
+                    nc.vector.scalar_tensor_tensor(
+                        out=z[:, bt, :], in0=z[:, bt, :], scalar=ALPHA, in1=z[:, bt, :], op0=ALU.mult, op1=ALU.max
+                    )
+                    nc.sync.dma_start(out=out_v[:, bt, li, :], in_=z[:, bt, :])
+            if not fine:
+                zf = z[:].rearrange("p t f -> p (t f)")
+                nc.vector.scalar_tensor_tensor(out=zf, in0=zf, scalar=ALPHA, in1=zf, op0=ALU.mult, op1=ALU.max)
+                nc.sync.dma_start(out=out_v[:, :, li, :], in_=z[:])
+
+        for k in range(8):
+            step(k)
+        for li in range(L):
+            k0 = TAPS * li + 8
+            if li < L - 1:
+                for ft in range(4):
+                    step(k0 + ft)
+                    new_acc(ft)
+                    for i in range(TAPS):
+                        mx_pass(li, ft, i)
+                    p1(li, ft)
+                step(k0 + 4)
+            else:
+                for ft in range(4):
+                    new_acc(ft)
+                for i in range(TAPS):
+                    for ft in range(4):
+                        mx_pass(li, ft, i)
+                for ft in range(4):
+                    p1(li, ft)
+            if li >= 1:
+                back(li - 1, False)
+        back(L - 1, True)

@@ -20,9 +20,15 @@ STEP = (0, 0, 1, -1, 2)
 BN_EPS = 1e-3
 ALPHA = 0.3
 N_CHUNKS = TAPS * L
-N_PAIRS = N_CHUNKS // 2
-RAW_BUFS = 6
-V_COLS = 192
+N_H = 8
+RAW_BUFS = 12
+V_COLS = 336
+QA = 1
+DP1 = 1
+DXT = 1
+DC = 3
+DM = 2
+X_AFTER = (9, 24)
 PIN = True
 
 
@@ -32,7 +38,7 @@ def tile_residualblock5_pb_t_kernel(tc, h, x, k2, b2, gamma2, beta2, mean2, var2
         const = ctx.enter_context(tc.tile_pool(name="const", bufs=1))
         rawp = ctx.enter_context(tc.tile_pool(name="rawp", bufs=RAW_BUFS))
         grpp = ctx.enter_context(tc.tile_pool(name="grpp", bufs=4))
-        kwp = ctx.enter_context(tc.tile_pool(name="kwp", bufs=8))
+        kwp = ctx.enter_context(tc.tile_pool(name="kwp", bufs=6))
         sp = ctx.enter_context(tc.tile_pool(name="sp", bufs=8))
         zpool = ctx.enter_context(tc.tile_pool(name="zpool", bufs=3))
         ps_a = ctx.enter_context(tc.psum_pool(name="ps_a", bufs=4))
@@ -54,29 +60,19 @@ def tile_residualblock5_pb_t_kernel(tc, h, x, k2, b2, gamma2, beta2, mean2, var2
         nc.scalar.dma_start(out=cst[16:48, :], in_=b2.rearrange("l (r c) -> (l r) c", c=P))
         nc.scalar.activation(out=warm[:], in_=warm[:], func=ACT.Sqrt)
         nc.vector.tensor_copy(out=ident_b[:], in_=ident_f[:])
+        c_t = const.tile([P, 48], F32, name="c_t")
+        t_var = const.tile([P, 4], F32, name="t_var")
+        t_std = const.tile([P, 4], F32, name="t_std")
+        t_rstd = const.tile([P, 4], F32, name="t_rstd")
+        a_sc = const.tile([P, 4], F32, name="a_sc")
+        b_sc = const.tile([P, L, 4], F32, name="b_sc")
+        hw = const.tile([P, L, 512], U32, name="hw", align_bytes=64)
+        hs = const.tile([P, L, 512], U8, name="hs", align_bytes=64)
 
         raws = {}
-        grps = {}
-        kws = {}
-        kss = {}
-
-        h_raw = []
-        for bt in range(4):
-            hr = rawp.tile([P, 4096], BF16, tag="raw", name="hraw")
-            nc.sync.dma_start(out=hr[:], in_=h[bt * P:(bt + 1) * P].rearrange("b l c -> b (l c)"))
-            h_raw.append(hr)
-
-        def load_pair(j):
-            rt = rawp.tile([P, 4096], BF16, tag="raw", name="kraw")
-            for hf in range(2):
-                li, i = divmod(2 * j + hf, TAPS)
-                nc.sync.dma_start(
-                    out=rt[:, hf * 2048:(hf + 1) * 2048],
-                    in_=k2[i, li].rearrange("(p t) f -> p (t f)", t=4),
-                )
-            raws[j] = rt
-
         xs = {}
+        units = [("h", u) for u in range(N_H)] + [("k", n) for n in range(N_CHUNKS)]
+        issued = [0]
 
         def load_x(half):
             for bt in range(4):
@@ -87,50 +83,169 @@ def tile_residualblock5_pb_t_kernel(tc, h, x, k2, b2, gamma2, beta2, mean2, var2
                 )
                 xs[(bt, half)] = xt
 
-        load_pair(0)
-        load_pair(1)
+        def issue():
+            if issued[0] >= len(units):
+                return
+            kind, idx = units[issued[0]]
+            issued[0] += 1
+            rt = rawp.tile([P, 2048], BF16, tag="raw", name="raw")
+            if kind == "h":
+                bt, half = divmod(idx, 2)
+                src = h[bt * P:(bt + 1) * P, half * 4:(half + 1) * 4, :].rearrange("b l c -> b (l c)")
+            else:
+                li, i = divmod(idx, TAPS)
+                src = k2[i, li].rearrange("(p t) f -> p (t f)", t=4)
+            nc.sync.dma_start(out=rt[:], in_=src)
+            raws[(kind, idx)] = rt
+            if kind == "k" and idx == X_AFTER[0]:
+                load_x(0)
+            if kind == "k" and idx == X_AFTER[1]:
+                load_x(1)
 
-        c_t = const.tile([P, 48], F32, name="c_t")
-        t_var = const.tile([P, 4], F32, name="t_var")
-        t_std = const.tile([P, 4], F32, name="t_std")
-        t_rstd = const.tile([P, 4], F32, name="t_rstd")
-        a_sc = const.tile([P, 4], F32, name="a_sc")
-        b_sc = const.tile([P, L, 4], F32, name="b_sc")
+        for r in range(RAW_BUFS):
+            issue()
 
-        hg = []
-        hw = []
-        hs = []
-        for mp in range(4):
-            hg.append(grpp.tile([P, 4096], BF16, tag="grp", name="hgrp", align_bytes=64))
-            hw.append(const.tile([P, 1024], U32, name="hw%d" % mp, align_bytes=64))
-            hs.append(const.tile([P, 1024], U8, name="hs%d" % mp, align_bytes=64))
+        hgs = {}
+        bank = [0]
 
-        for bt in range(4):
-            hv = h_raw[bt][:].bitcast(F32).rearrange("b (m p u) -> b m u p", p=P, u=2)
-            for mp in range(4):
-                if mp % 2 == 0:
+        def h_evacuate(u):
+            hg = grpp.tile([P, 2048], BF16, tag="grp", name="hgrp", align_bytes=64)
+            hgs[u] = hg
+            hv = raws[("h", u)][:].bitcast(F32).rearrange("b (m p u) -> b m u p", p=P, u=2)
+            for mp in range(2):
+                if bank[0] % 2 == 0:
                     tp = ps_a.tile([P, 2, 2, P], F32, tag="acc", name="tp_a")
                 else:
                     tp = ps_b.tile([P, 2, 2, P], F32, tag="zp", name="tp_b")
+                bank[0] += 1
                 for mi in range(2):
-                    for u in range(2):
-                        nc.tensor.transpose(tp[:, mi, u, :], hv[:, 2 * mp + mi, u, :], ident_f[:])
-                dst = hg[mp][:].bitcast(F32).rearrange("p (m b u) -> p m b u", m=2, u=2)[:, :, bt * P:(bt + 1) * P, :]
-                src = tp[:].rearrange("p m u b -> p m b u")
-                if mp % 2 == 0:
-                    nc.vector.tensor_copy(out=dst, in_=src)
+                    for w in range(2):
+                        nc.tensor.transpose(tp[:, mi, w, :], hv[:, 2 * mp + mi, w, :], ident_f[:])
+                dst = hg[:].bitcast(F32)[:, mp * 512:(mp + 1) * 512].rearrange("p (m b u) -> p m b u", m=2, u=2)
+                nc.scalar.copy(out=dst, in_=tp[:].rearrange("p m u b -> p m b u"))
+            issue()
+
+        def h_quantise(u):
+            bt, half = divmod(u, 2)
+            for m in range(4):
+                nc.vector.quantize_mx(
+                    out=hw[:, half * 4 + m, bt * P:(bt + 1) * P].bitcast(FP8X4),
+                    scales=hs[:, half * 4 + m, bt * P:(bt + 1) * P],
+                    in_=hgs[u][:, m * 512:(m + 1) * 512],
+                )
+
+        grps = {}
+        kws = {}
+        kss = {}
+        accs = {}
+        s_tiles = {}
+        zps = {}
+        zs = {}
+        pending = []
+        bn_done = set()
+
+        def regroup(n):
+            g = grpp.tile([P, 2048], BF16, tag="grp", name="kgrp", align_bytes=64)
+            grps[n] = g
+            src = raws[("k", n)][:].rearrange("p (t c i) -> p c t i", t=4, i=4)
+            dst = g[:].rearrange("p (c i t) -> p c t i", i=4, t=4)
+            cv = V_COLS // 4
+            nc.vector.tensor_copy(out=dst[:, 0:cv], in_=src[:, 0:cv])
+            nc.scalar.copy(out=dst[:, cv:], in_=src[:, cv:])
+            issue()
+
+        def quantise(n):
+            kws[n] = kwp.tile([P, 512], U32, tag="kw", name="kw", align_bytes=64)
+            kss[n] = kwp.tile([P, 512], U8, tag="ks", name="ks", align_bytes=64)
+            nc.vector.quantize_mx(out=kws[n][:].bitcast(FP8X4), scales=kss[n][:], in_=grps[n][:])
+            pending.append(n)
+
+        def flush_mx():
+            while len(pending) > 0:
+                n = pending[0]
+                li, i = divmod(n, TAPS)
+                if i == 0 and li > 0 and (li - 1) not in bn_done:
+                    break
+                pending.pop(0)
+                if i == 0:
+                    for ft in range(4):
+                        accs[(li, ft)] = ps_a.tile([P, 512], F32, tag="acc", name="acc")
+                m = (li - STEP[i]) % L
+                for ft in range(4):
+                    nc.tensor.matmul_mx(
+                        out=accs[(li, ft)][:],
+                        lhsT=kws[n][:, ft * P:(ft + 1) * P].bitcast(FP8X4),
+                        lhsT_scale=kss[n][:, ft * P:(ft + 1) * P],
+                        rhs=hw[:, m, :].bitcast(FP8X4),
+                        rhs_scale=hs[:, m, :],
+                        start=(i == 0),
+                        stop=(i == TAPS - 1),
+                    )
+
+        def batch_norm(li):
+            flush_mx()
+            bn_done.add(li)
+            for ft in range(4):
+                st = sp.tile([P, 512], F32, tag="s", name="s")
+                if li == L - 1 and ft % 2 == 1:
+                    nc.vector.tensor_scalar(
+                        out=st[:], in0=accs[(li, ft)][:], scalar1=a_sc[:, ft:ft + 1],
+                        scalar2=b_sc[:, li, ft:ft + 1], op0=ALU.mult, op1=ALU.add,
+                    )
                 else:
-                    nc.scalar.copy(out=dst, in_=src)
-            load_pair(2 + bt)
-            if bt == 0:
+                    nc.scalar.activation(
+                        out=st[:], in_=accs[(li, ft)][:], func=ACT.Identity,
+                        scale=a_sc[:, ft:ft + 1], bias=b_sc[:, li, ft:ft + 1],
+                    )
+                s_tiles[(li, ft)] = st
+
+        def back(li):
+            for bt in range(4):
+                zp = ps_b.tile([P, 512], F32, tag="zp", name="zp")
+                zps[(li, bt)] = zp
+                xt = xs[(bt, li // 4)]
+                nc.tensor.matmul(
+                    out=zp[:], lhsT=ident_b[:], rhs=xt[:, (li % 4) * 512:(li % 4 + 1) * 512], start=True, stop=False
+                )
+                for ft in range(4):
+                    nc.tensor.matmul(
+                        out=zp[:, ft * P:(ft + 1) * P],
+                        lhsT=s_tiles[(li, ft)][:, bt * P:(bt + 1) * P],
+                        rhs=ident_f[:],
+                        is_transpose=True,
+                        start=False,
+                        stop=(ft == 3),
+                    )
+
+        def copy_out(li):
+            zs[li] = zpool.tile([P, 4, 512], F32, tag="z", name="z")
+            for bt in range(4):
+                nc.scalar.copy(out=zs[li][:, bt, :], in_=zps[(li, bt)][:])
+
+        out_v = out.rearrange("(t p) l f -> p t l f", p=P)
+
+        def leaky_store(li):
+            z = zs[li]
+            if li == L - 1:
+                for bt in range(4):
+                    nc.vector.scalar_tensor_tensor(
+                        out=z[:, bt, :], in0=z[:, bt, :], scalar=ALPHA, in1=z[:, bt, :], op0=ALU.mult, op1=ALU.max
+                    )
+                    nc.sync.dma_start(out=out_v[:, bt, li, :], in_=z[:, bt, :])
+            else:
+                zf = z[:].rearrange("p t f -> p (t f)")
+                nc.vector.scalar_tensor_tensor(out=zf, in0=zf, scalar=ALPHA, in1=zf, op0=ALU.mult, op1=ALU.max)
+                nc.sync.dma_start(out=out_v[:, :, li, :], in_=z[:])
+
+        def bn_constants(k):
+            if k == 0:
                 cps = ps_b.tile([P, P], BF16, tag="zp", name="cps")
                 nc.tensor.transpose(cps[:], cst[:], ident_b[:])
                 nc.vector.tensor_copy(out=c_t[:], in_=cps[:, 0:48])
                 nc.vector.tensor_scalar(out=t_var[:], in0=c_t[:, 12:16], scalar1=BN_EPS, scalar2=None, op0=ALU.add)
-            if bt == 1:
+            if k == 1:
                 nc.scalar.activation(out=t_std[:], in_=t_var[:], func=ACT.Sqrt)
-            if bt == 2:
-                load_x(0)
+            if k == 2:
                 nc.vector.reciprocal(out=t_rstd[:], in_=t_std[:])
                 nc.vector.tensor_tensor(out=a_sc[:], in0=t_rstd[:], in1=c_t[:, 0:4], op=ALU.mult)
                 nc.vector.scalar_tensor_tensor(
@@ -147,109 +262,25 @@ def tile_residualblock5_pb_t_kernel(tc, h, x, k2, b2, gamma2, beta2, mean2, var2
                 nc.vector.tensor_tensor(
                     out=b_sc[:], in0=b_sc[:], in1=c_t[:, 4:8].unsqueeze(1).to_broadcast([P, L, 4]), op=ALU.add
                 )
-        for mp in range(4):
-            nc.vector.quantize_mx(out=hw[mp][:].bitcast(FP8X4), scales=hs[mp][:], in_=hg[mp][:])
 
-        def regroup(n):
-            j, hf = divmod(n, 2)
-            if hf == 0:
-                grps[j] = grpp.tile([P, 4096], BF16, tag="grp", name="kgrp", align_bytes=64)
-            src = raws[j][:, hf * 2048:(hf + 1) * 2048].rearrange("p (t c i) -> p c t i", t=4, i=4)
-            dst = grps[j][:, hf * 2048:(hf + 1) * 2048].rearrange("p (c i t) -> p c t i", i=4, t=4)
-            cv = V_COLS // 4
-            nc.vector.tensor_copy(out=dst[:, 0:cv], in_=src[:, 0:cv])
-            nc.scalar.copy(out=dst[:, cv:], in_=src[:, cv:])
-
-        def quantise(j):
-            kws[j] = kwp.tile([P, 1024], U32, tag="kw", name="kw", align_bytes=64)
-            kss[j] = kwp.tile([P, 1024], U8, tag="ks", name="ks", align_bytes=64)
-            nc.vector.quantize_mx(out=kws[j][:].bitcast(FP8X4), scales=kss[j][:], in_=grps[j][:])
-
-        def step(k):
-            if k < N_CHUNKS:
-                regroup(k)
-                if k % 2 == 1:
-                    j = (k - 1) // 2 + RAW_BUFS
-                    if j < N_PAIRS:
-                        load_pair(j)
-                    if j == 16:
-                        load_x(1)
-            if k >= 3 and k % 2 == 1 and (k - 3) // 2 < N_PAIRS:
-                quantise((k - 3) // 2)
-
-        accs = {}
-        s_tiles = {}
-
-        def mx_pass(li, ft, i):
-            m = (li - STEP[i]) % L
-            j, hf = divmod(TAPS * li + i, 2)
-            kc = slice(hf * 512 + ft * P, hf * 512 + (ft + 1) * P)
-            hc = slice((m % 2) * 512, (m % 2) * 512 + 512)
-            nc.tensor.matmul_mx(
-                out=accs[ft][:],
-                lhsT=kws[j][:, kc].bitcast(FP8X4),
-                lhsT_scale=kss[j][:, kc],
-                rhs=hw[m // 2][:, hc].bitcast(FP8X4),
-                rhs_scale=hs[m // 2][:, hc],
-                start=(i == 0),
-                stop=(i == TAPS - 1),
-            )
-
-        def new_acc(ft):
-            accs[ft] = ps_a.tile([P, 512], F32, tag="acc", name="acc")
-
-        def p1(li, ft):
-            st = sp.tile([P, 512], F32, tag="s", name="s")
-            nc.scalar.activation(
-                out=st[:], in_=accs[ft][:], func=ACT.Identity,
-                scale=a_sc[:, ft:ft + 1], bias=b_sc[:, li, ft:ft + 1],
-            )
-            s_tiles[(li, ft)] = st
-
-        out_v = out.rearrange("(t p) l f -> p t l f", p=P)
-
-        def back(li, fine):
-            z = zpool.tile([P, 4, 512], F32, tag="z", name="z")
-            for bt in range(4):
-                zp = ps_b.tile([P, 512], F32, tag="zp", name="zp")
-                for ft in range(4):
-                    nc.tensor.transpose(
-                        zp[:, ft * P:(ft + 1) * P], s_tiles[(li, ft)][:, bt * P:(bt + 1) * P], ident_f[:]
-                    )
-                xt = xs[(bt, li // 4)]
-                nc.vector.tensor_tensor(
-                    out=z[:, bt, :], in0=zp[:], in1=xt[:, (li % 4) * 512:(li % 4 + 1) * 512], op=ALU.add
-                )
-                if fine:
-                    nc.vector.scalar_tensor_tensor(
-                        out=z[:, bt, :], in0=z[:, bt, :], scalar=ALPHA, in1=z[:, bt, :], op0=ALU.mult, op1=ALU.max
-                    )
-                    nc.sync.dma_start(out=out_v[:, bt, li, :], in_=z[:, bt, :])
-            if not fine:
-                zf = z[:].rearrange("p t f -> p (t f)")
-                nc.vector.scalar_tensor_tensor(out=zf, in0=zf, scalar=ALPHA, in1=zf, op0=ALU.mult, op1=ALU.max)
-                nc.sync.dma_start(out=out_v[:, :, li, :], in_=z[:])
-
-        for k in range(8):
-            step(k)
-        for li in range(L):
-            k0 = TAPS * li + 8
-            if li < L - 1:
-                for ft in range(4):
-                    step(k0 + ft)
-                    new_acc(ft)
-                    for i in range(TAPS):
-                        mx_pass(li, ft, i)
-                    p1(li, ft)
-                step(k0 + 4)
-            else:
-                for ft in range(4):
-                    new_acc(ft)
-                for i in range(TAPS):
-                    for ft in range(4):
-                        mx_pass(li, ft, i)
-                for ft in range(4):
-                    p1(li, ft)
-            if li >= 1:
-                back(li - 1, False)
-        back(L - 1, True)
+        for k in range(N_H + N_CHUNKS + QA + DP1 + DC + DM + 1):
+            if k < N_H:
+                h_evacuate(k)
+            elif k < N_H + N_CHUNKS:
+                regroup(k - N_H)
+            bn_constants(k)
+            if 0 <= k - N_H - QA < N_CHUNKS:
+                quantise(k - N_H - QA)
+            if 1 <= k <= N_H:
+                h_quantise(k - 1)
+            for li in range(L):
+                s0 = N_H + TAPS * li + TAPS - 1 + QA + DP1
+                if k == s0:
+                    batch_norm(li)
+                if k == s0 + DXT:
+                    back(li)
+                if k == s0 + DC:
+                    copy_out(li)
+                if k == s0 + DC + DM:
+                    leaky_store(li)
+            flush_mx()

@@ -29,7 +29,7 @@ DXT = 1
 DC = 3
 DM = 2
 X_AFTER = (9, 24)
-PIN = True
+PIN = False
 
 
 def tile_residualblock5_pb_t_kernel(tc, h, x, k2, b2, gamma2, beta2, mean2, var2, out):
@@ -207,9 +207,10 @@ def tile_residualblock5_pb_t_kernel(tc, h, x, k2, b2, gamma2, beta2, mean2, var2
                 nc.tensor.matmul(
                     out=zp[:], lhsT=ident_b[:], rhs=xt[:, (li % 4) * 512:(li % 4 + 1) * 512], start=True, stop=False
                 )
+            for bt in range(4):
                 for ft in range(4):
                     nc.tensor.matmul(
-                        out=zp[:, ft * P:(ft + 1) * P],
+                        out=zps[(li, bt)][:, ft * P:(ft + 1) * P],
                         lhsT=s_tiles[(li, ft)][:, bt * P:(bt + 1) * P],
                         rhs=ident_f[:],
                         is_transpose=True,

@@ -20,16 +20,16 @@ STEP = (0, 0, 1, -1, 2)
 BN_EPS = 1e-3
 ALPHA = 0.3
 N_CHUNKS = TAPS * L
-N_H = 8
-RAW_BUFS = 12
+ORDER = (2, 3, 4, 5, 6, 7, 0, 1)
+RAW_BUFS = 10
 V_COLS = 336
-QA = 1
-DP1 = 1
-DXT = 1
-DC = 3
-DM = 2
-X_AFTER = (9, 24)
-PIN = False
+PIN = True
+HEAD = (
+    "k0 h0 k1 h1 k2 h2 k3 h3 k4 k5 h4 k6 h5 k7 x0 k8 k9 k10 h6 k11 h7 k12 k13 k14 x1 k15 k16 k17 k18 k19 k20 k21 k22 k23"
+    " k24 x2 k25 k26 k27 k28 k29 k30 k31 k32 k33 k34 x3 k35 k36 k37 k38 k39"
+)
+M_PAIRS = (2, 0, 4, 6)
+LAG_FROM = 6
 
 
 def tile_residualblock5_pb_t_kernel(tc, h, x, k2, b2, gamma2, beta2, mean2, var2, out):
@@ -37,14 +37,60 @@ def tile_residualblock5_pb_t_kernel(tc, h, x, k2, b2, gamma2, beta2, mean2, var2
     with ExitStack() as ctx:
         const = ctx.enter_context(tc.tile_pool(name="const", bufs=1))
         rawp = ctx.enter_context(tc.tile_pool(name="rawp", bufs=RAW_BUFS))
-        grpp = ctx.enter_context(tc.tile_pool(name="grpp", bufs=4))
-        kwp = ctx.enter_context(tc.tile_pool(name="kwp", bufs=6))
+        grpp = ctx.enter_context(tc.tile_pool(name="grpp", bufs=5))
+        kwp = ctx.enter_context(tc.tile_pool(name="kwp", bufs=8))
+        hgp = ctx.enter_context(tc.tile_pool(name="hgp", bufs=2))
         sp = ctx.enter_context(tc.tile_pool(name="sp", bufs=8))
-        zpool = ctx.enter_context(tc.tile_pool(name="zpool", bufs=3))
+        zpool = ctx.enter_context(tc.tile_pool(name="zpool", bufs=4))
         ps_a = ctx.enter_context(tc.psum_pool(name="ps_a", bufs=4))
         ps_b = ctx.enter_context(tc.psum_pool(name="ps_b", bufs=4))
         if PIN:
             ctx.enter_context(tc.manual_schedule())
+
+        loads = []
+        for word in HEAD.split():
+            loads.append((word[0], int(word[1:])))
+        raws = {}
+        xs = {}
+        issued = [0, 0]
+
+        def taps_of(j):
+            return (0, 1, 3, 2, 4) if j == 0 else (0, 1, 2, 4, 3)
+
+        def issue():
+            while issued[0] < len(loads):
+                kind, idx = loads[issued[0]]
+                if kind == "x":
+                    l0 = ORDER[2 * idx]
+                    xt = const.tile([P, 4, 1024], BF16, name="x_%d" % idx)
+                    nc.sync.dma_start(
+                        out=xt[:], in_=x.rearrange("(t p) l f -> p t (l f)", p=P)[:, :, l0 * 512:(l0 + 2) * 512]
+                    )
+                    xs[l0] = xt
+                    issued[0] += 1
+                    continue
+                if kind == "h":
+                    pair, bh = divmod(idx, 2)
+                    m0 = M_PAIRS[pair]
+                    ht = const.tile([P, 2, 1024], BF16, name="h_%d" % idx)
+                    nc.sync.dma_start(
+                        out=ht[:],
+                        in_=h.rearrange("(t p) l c -> p t (l c)", p=P)[:, 2 * bh:2 * bh + 2, m0 * 512:(m0 + 2) * 512],
+                    )
+                    raws[("h", idx)] = ht
+                    issued[0] += 1
+                    continue
+                if issued[1] >= RAW_BUFS + freed[0]:
+                    return
+                rt = rawp.tile([P, 2048], BF16, tag="raw", name="raw")
+                j, i = divmod(idx, TAPS)
+                nc.sync.dma_start(out=rt[:], in_=k2[taps_of(j)[i], ORDER[j]].rearrange("(p t) f -> p (t f)", t=4))
+                raws[("k", idx)] = rt
+                issued[0] += 1
+                issued[1] += 1
+
+        freed = [0]
+        issue()
 
         ident_f = const.tile([P, P], F32, name="ident_f")
         make_identity(nc, ident_f[:])
@@ -69,72 +115,29 @@ def tile_residualblock5_pb_t_kernel(tc, h, x, k2, b2, gamma2, beta2, mean2, var2
         hw = const.tile([P, L, 512], U32, name="hw", align_bytes=64)
         hs = const.tile([P, L, 512], U8, name="hs", align_bytes=64)
 
-        raws = {}
-        xs = {}
-        units = [("h", u) for u in range(N_H)] + [("k", n) for n in range(N_CHUNKS)]
-        issued = [0]
-
-        def load_x(half):
-            for bt in range(4):
-                xt = const.tile([P, 2048], BF16, name="x_%d_%d" % (bt, half))
-                nc.sync.dma_start(
-                    out=xt[:],
-                    in_=x[bt * P:(bt + 1) * P, half * 4:(half + 1) * 4, :].rearrange("b l f -> b (l f)"),
-                )
-                xs[(bt, half)] = xt
-
-        def issue():
-            if issued[0] >= len(units):
-                return
-            kind, idx = units[issued[0]]
-            issued[0] += 1
-            rt = rawp.tile([P, 2048], BF16, tag="raw", name="raw")
-            if kind == "h":
-                bt, half = divmod(idx, 2)
-                src = h[bt * P:(bt + 1) * P, half * 4:(half + 1) * 4, :].rearrange("b l c -> b (l c)")
-            else:
-                li, i = divmod(idx, TAPS)
-                src = k2[i, li].rearrange("(p t) f -> p (t f)", t=4)
-            nc.sync.dma_start(out=rt[:], in_=src)
-            raws[(kind, idx)] = rt
-            if kind == "k" and idx == X_AFTER[0]:
-                load_x(0)
-            if kind == "k" and idx == X_AFTER[1]:
-                load_x(1)
-
-        for r in range(RAW_BUFS):
-            issue()
-
-        hgs = {}
-        bank = [0]
-
-        def h_evacuate(u):
-            hg = grpp.tile([P, 2048], BF16, tag="grp", name="hgrp", align_bytes=64)
-            hgs[u] = hg
-            hv = raws[("h", u)][:].bitcast(F32).rearrange("b (m p u) -> b m u p", p=P, u=2)
-            for mp in range(2):
-                if bank[0] % 2 == 0:
-                    tp = ps_a.tile([P, 2, 2, P], F32, tag="acc", name="tp_a")
-                else:
-                    tp = ps_b.tile([P, 2, 2, P], F32, tag="zp", name="tp_b")
-                bank[0] += 1
-                for mi in range(2):
-                    for w in range(2):
-                        nc.tensor.transpose(tp[:, mi, w, :], hv[:, 2 * mp + mi, w, :], ident_f[:])
-                dst = hg[:].bitcast(F32)[:, mp * 512:(mp + 1) * 512].rearrange("p (m b u) -> p m b u", m=2, u=2)
-                nc.scalar.copy(out=dst, in_=tp[:].rearrange("p m u b -> p m b u"))
-            issue()
-
-        def h_quantise(u):
-            bt, half = divmod(u, 2)
-            for m in range(4):
-                nc.vector.quantize_mx(
-                    out=hw[:, half * 4 + m, bt * P:(bt + 1) * P].bitcast(FP8X4),
-                    scales=hs[:, half * 4 + m, bt * P:(bt + 1) * P],
-                    in_=hgs[u][:, m * 512:(m + 1) * 512],
-                )
-
         grps = {}
+        h_done = set()
+
+        def h_evacuate(u, mi):
+            pair, bh = divmod(u, 2)
+            m = M_PAIRS[pair] + mi
+            if bh == 0:
+                grps[("h", m)] = hgp.tile([P, 2048], BF16, tag="hg", name="hg", align_bytes=64)
+            hv = raws[("h", u)][:].rearrange("b t c -> b (t c)").bitcast(F32)
+            hv = hv.rearrange("b (t m p u) -> b t m u p", t=2, m=2, u=2)
+            tp = ps_b.tile([P, 2, 2, P], F32, tag="zp", name="tp")
+            for t in range(2):
+                for w in range(2):
+                    nc.tensor.transpose(tp[:, t, w, :], hv[:, t, mi, w, :], ident_f[:])
+            dst = grps[("h", m)][:].bitcast(F32)[:, bh * 512:(bh + 1) * 512]
+            nc.scalar.copy(
+                out=dst.rearrange("p (t b u) -> p t b u", t=2, u=2), in_=tp[:].rearrange("p t u b -> p t b u")
+            )
+
+        def h_quantise(m):
+            nc.vector.quantize_mx(out=hw[:, m, :].bitcast(FP8X4), scales=hs[:, m, :], in_=grps[("h", m)][:])
+            h_done.add(m)
+
         kws = {}
         kss = {}
         accs = {}
@@ -146,34 +149,35 @@ def tile_residualblock5_pb_t_kernel(tc, h, x, k2, b2, gamma2, beta2, mean2, var2
 
         def regroup(n):
             g = grpp.tile([P, 2048], BF16, tag="grp", name="kgrp", align_bytes=64)
-            grps[n] = g
+            grps[("k", n)] = g
             src = raws[("k", n)][:].rearrange("p (t c i) -> p c t i", t=4, i=4)
             dst = g[:].rearrange("p (c i t) -> p c t i", i=4, t=4)
             cv = V_COLS // 4
             nc.vector.tensor_copy(out=dst[:, 0:cv], in_=src[:, 0:cv])
             nc.scalar.copy(out=dst[:, cv:], in_=src[:, cv:])
-            issue()
 
         def quantise(n):
             kws[n] = kwp.tile([P, 512], U32, tag="kw", name="kw", align_bytes=64)
             kss[n] = kwp.tile([P, 512], U8, tag="ks", name="ks", align_bytes=64)
-            nc.vector.quantize_mx(out=kws[n][:].bitcast(FP8X4), scales=kss[n][:], in_=grps[n][:])
+            nc.vector.quantize_mx(out=kws[n][:].bitcast(FP8X4), scales=kss[n][:], in_=grps[("k", n)][:])
             pending.append(n)
 
         def flush_mx():
             while len(pending) > 0:
                 n = pending[0]
-                li, i = divmod(n, TAPS)
-                if i == 0 and li > 0 and (li - 1) not in bn_done:
+                j, i = divmod(n, TAPS)
+                m = (ORDER[j] - STEP[taps_of(j)[i]]) % L
+                if i == 0 and j > 0 and (j - 1) not in bn_done:
+                    break
+                if m not in h_done:
                     break
                 pending.pop(0)
                 if i == 0:
                     for ft in range(4):
-                        accs[(li, ft)] = ps_a.tile([P, 512], F32, tag="acc", name="acc")
-                m = (li - STEP[i]) % L
+                        accs[(j, ft)] = ps_a.tile([P, 512], F32, tag="acc", name="acc")
                 for ft in range(4):
                     nc.tensor.matmul_mx(
-                        out=accs[(li, ft)][:],
+                        out=accs[(j, ft)][:],
                         lhsT=kws[n][:, ft * P:(ft + 1) * P].bitcast(FP8X4),
                         lhsT_scale=kss[n][:, ft * P:(ft + 1) * P],
                         rhs=hw[:, m, :].bitcast(FP8X4),
@@ -182,61 +186,63 @@ def tile_residualblock5_pb_t_kernel(tc, h, x, k2, b2, gamma2, beta2, mean2, var2
                         stop=(i == TAPS - 1),
                     )
 
-        def batch_norm(li):
-            flush_mx()
-            bn_done.add(li)
+        def batch_norm(j):
+            bn_done.add(j)
             for ft in range(4):
                 st = sp.tile([P, 512], F32, tag="s", name="s")
-                if li == L - 1 and ft % 2 == 1:
+                if j == L - 1 and ft % 2 == 1:
                     nc.vector.tensor_scalar(
-                        out=st[:], in0=accs[(li, ft)][:], scalar1=a_sc[:, ft:ft + 1],
-                        scalar2=b_sc[:, li, ft:ft + 1], op0=ALU.mult, op1=ALU.add,
+                        out=st[:], in0=accs[(j, ft)][:], scalar1=a_sc[:, ft:ft + 1],
+                        scalar2=b_sc[:, ORDER[j], ft:ft + 1], op0=ALU.mult, op1=ALU.add,
                     )
                 else:
                     nc.scalar.activation(
-                        out=st[:], in_=accs[(li, ft)][:], func=ACT.Identity,
-                        scale=a_sc[:, ft:ft + 1], bias=b_sc[:, li, ft:ft + 1],
+                        out=st[:], in_=accs[(j, ft)][:], func=ACT.Identity,
+                        scale=a_sc[:, ft:ft + 1], bias=b_sc[:, ORDER[j], ft:ft + 1],
                     )
-                s_tiles[(li, ft)] = st
+                s_tiles[(j, ft)] = st
 
-        def back(li):
+        def add_x(j):
+            l0 = ORDER[j] // 2 * 2
             for bt in range(4):
                 zp = ps_b.tile([P, 512], F32, tag="zp", name="zp")
-                zps[(li, bt)] = zp
-                xt = xs[(bt, li // 4)]
+                zps[(j, bt)] = zp
+                lo = (ORDER[j] - l0) * 512
                 nc.tensor.matmul(
-                    out=zp[:], lhsT=ident_b[:], rhs=xt[:, (li % 4) * 512:(li % 4 + 1) * 512], start=True, stop=False
+                    out=zp[:], lhsT=ident_b[:], rhs=xs[l0][:, bt, lo:lo + 512], start=True, stop=False
                 )
-            for bt in range(4):
-                for ft in range(4):
+
+        def back(j):
+            for ft in range(4):
+                for bt in range(4):
                     nc.tensor.matmul(
-                        out=zps[(li, bt)][:, ft * P:(ft + 1) * P],
-                        lhsT=s_tiles[(li, ft)][:, bt * P:(bt + 1) * P],
+                        out=zps[(j, bt)][:, ft * P:(ft + 1) * P],
+                        lhsT=s_tiles[(j, ft)][:, bt * P:(bt + 1) * P],
                         rhs=ident_f[:],
                         is_transpose=True,
                         start=False,
                         stop=(ft == 3),
                     )
 
-        def copy_out(li):
-            zs[li] = zpool.tile([P, 4, 512], F32, tag="z", name="z")
-            for bt in range(4):
-                nc.scalar.copy(out=zs[li][:, bt, :], in_=zps[(li, bt)][:])
+        def copy_out(j, pair):
+            zs[(j, pair)] = zpool.tile([P, 2, 512], F32, tag="z", name="z")
+            for q in range(2):
+                nc.scalar.copy(out=zs[(j, pair)][:, q, :], in_=zps[(j, 2 * pair + q)][:])
 
         out_v = out.rearrange("(t p) l f -> p t l f", p=P)
 
-        def leaky_store(li):
-            z = zs[li]
-            if li == L - 1:
-                for bt in range(4):
+        def leaky_store(j, pair):
+            z = zs[(j, pair)]
+            if j == L - 1:
+                for q in range(2):
                     nc.vector.scalar_tensor_tensor(
-                        out=z[:, bt, :], in0=z[:, bt, :], scalar=ALPHA, in1=z[:, bt, :], op0=ALU.mult, op1=ALU.max
+                        out=z[:, q, :], in0=z[:, q, :], scalar=ALPHA, in1=z[:, q, :], op0=ALU.mult, op1=ALU.max
                     )
-                    nc.sync.dma_start(out=out_v[:, bt, li, :], in_=z[:, bt, :])
+                    nc.sync.dma_start(out=out_v[:, 2 * pair + q, ORDER[j], :], in_=z[:, q, :])
             else:
                 zf = z[:].rearrange("p t f -> p (t f)")
                 nc.vector.scalar_tensor_tensor(out=zf, in0=zf, scalar=ALPHA, in1=zf, op0=ALU.mult, op1=ALU.max)
-                nc.sync.dma_start(out=out_v[:, :, li, :], in_=z[:])
+                nc.sync.dma_start(out=out_v[:, 2 * pair:2 * pair + 2, ORDER[j], :], in_=z[:])
 
         def bn_constants(k):
             if k == 0:
@@ -257,31 +263,49 @@ def tile_residualblock5_pb_t_kernel(tc, h, x, k2, b2, gamma2, beta2, mean2, var2
                     op0=ALU.mult,
                     op1=ALU.subtract,
                 )
+            if k == 3:
                 nc.vector.tensor_tensor(
                     out=b_sc[:], in0=b_sc[:], in1=a_sc[:].unsqueeze(1).to_broadcast([P, L, 4]), op=ALU.mult
                 )
+            if k == 4:
                 nc.vector.tensor_tensor(
                     out=b_sc[:], in0=b_sc[:], in1=c_t[:, 4:8].unsqueeze(1).to_broadcast([P, L, 4]), op=ALU.add
                 )
 
-        for k in range(N_H + N_CHUNKS + QA + DP1 + DC + DM + 1):
-            if k < N_H:
-                h_evacuate(k)
-            elif k < N_H + N_CHUNKS:
-                regroup(k - N_H)
-            bn_constants(k)
-            if 0 <= k - N_H - QA < N_CHUNKS:
-                quantise(k - N_H - QA)
-            if 1 <= k <= N_H:
-                h_quantise(k - 1)
-            for li in range(L):
-                s0 = N_H + TAPS * li + TAPS - 1 + QA + DP1
-                if k == s0:
-                    batch_norm(li)
-                if k == s0 + DXT:
-                    back(li)
-                if k == s0 + DC:
-                    copy_out(li)
-                if k == s0 + DC + DM:
-                    leaky_store(li)
+        h_evac = {0: [(0, 0), (0, 1)], 1: [(1, 0), (1, 1)], 2: [(2, 0), (2, 1)], 3: [(3, 0), (3, 1)],
+                  9: [(4, 0), (5, 0)], 10: [(4, 1), (5, 1)], 16: [(6, 0), (7, 0)], 21: [(6, 1), (7, 1)]}
+        h_quant = {2: [2, 3], 4: [1, 0], 10: [4], 11: [5], 17: [6], 22: [7]}
+        for n in range(N_CHUNKS + 8):
+            if n < N_CHUNKS:
+                regroup(n)
+                freed[0] += 1
+                issue()
+            for u, mi in h_evac.get(n, []):
+                h_evacuate(u, mi)
+            for m in h_quant.get(n, []):
+                h_quantise(m)
+            if 1 <= n < LAG_FROM:
+                quantise(n - 1)
+            elif LAG_FROM < n < N_CHUNKS:
+                quantise(n - 2)
+            elif n == N_CHUNKS:
+                quantise(n - 2)
+                quantise(n - 1)
+            bn_constants(n - 2)
+            for j in range(L):
+                e = TAPS * j + TAPS - 1 + (1 if LAG_FROM < TAPS * j + TAPS < N_CHUNKS else 0)
+                if n == e + 2:
+                    batch_norm(j)
+                    back(j)
+                if n == e + 4:
+                    copy_out(j, 0)
+                    copy_out(j, 1)
+                if n == e + 5:
+                    leaky_store(j, 0)
+                if n == e + 6:
+                    leaky_store(j, 1)
             flush_mx()
+            for j in range(L):
+                e = TAPS * j + TAPS - 1 + (1 if LAG_FROM < TAPS * j + TAPS < N_CHUNKS else 0)
+                if n == e + 1:
+                    add_x(j)

@@ -22,14 +22,15 @@ ALPHA = 0.3
 N_CHUNKS = TAPS * L
 ORDER = (2, 3, 4, 5, 6, 7, 0, 1)
 RAW_BUFS = 10
-V_COLS = 336
-PIN = True
-HEAD = (
-    "k0 h0 k1 h1 k2 h2 k3 h3 k4 k5 h4 k6 h5 k7 x0 k8 k9 k10 h6 k11 h7 k12 k13 k14 x1 k15 k16 k17 k18 k19 k20 k21 k22 k23"
-    " k24 x2 k25 k26 k27 k28 k29 k30 k31 k32 k33 k34 x3 k35 k36 k37 k38 k39"
+V_COLS = 328
+V_TAIL = 416
+PIN = False
+LOADS = (
+    "k0 h0 k1 h1 k2 h2 k3 h3 k4 k5 h4 k6 h5 k7 k8 k9 x0 k10 k11 k12 k13 k14 k15 k16 k17 h6 k18 h7 k19 k20 x1 k21 k22 k23"
+    " k24 k25 k26 k27 k28 k29 k30 x2 k31 k32 k33 k34 k35 k36 k37 k38 k39 x3"
 )
 M_PAIRS = (2, 0, 4, 6)
-LAG_FROM = 6
+LAG2_FROM = 5
 
 
 def tile_residualblock5_pb_t_kernel(tc, h, x, k2, b2, gamma2, beta2, mean2, var2, out):
@@ -38,17 +39,17 @@ def tile_residualblock5_pb_t_kernel(tc, h, x, k2, b2, gamma2, beta2, mean2, var2
         const = ctx.enter_context(tc.tile_pool(name="const", bufs=1))
         rawp = ctx.enter_context(tc.tile_pool(name="rawp", bufs=RAW_BUFS))
         grpp = ctx.enter_context(tc.tile_pool(name="grpp", bufs=5))
-        kwp = ctx.enter_context(tc.tile_pool(name="kwp", bufs=8))
+        kwp = ctx.enter_context(tc.tile_pool(name="kwp", bufs=10))
         hgp = ctx.enter_context(tc.tile_pool(name="hgp", bufs=2))
         sp = ctx.enter_context(tc.tile_pool(name="sp", bufs=8))
-        zpool = ctx.enter_context(tc.tile_pool(name="zpool", bufs=4))
+        zpool = ctx.enter_context(tc.tile_pool(name="zpool", bufs=3))
         ps_a = ctx.enter_context(tc.psum_pool(name="ps_a", bufs=4))
         ps_b = ctx.enter_context(tc.psum_pool(name="ps_b", bufs=4))
         if PIN:
             ctx.enter_context(tc.manual_schedule())
 
         loads = []
-        for word in HEAD.split():
+        for word in LOADS.split():
             loads.append((word[0], int(word[1:])))
         raws = {}
         xs = {}
@@ -118,17 +119,24 @@ def tile_residualblock5_pb_t_kernel(tc, h, x, k2, b2, gamma2, beta2, mean2, var2
         grps = {}
         h_done = set()
 
-        def h_evacuate(u, mi):
+        tps = {}
+
+        def h_transpose(u, mi):
             pair, bh = divmod(u, 2)
-            m = M_PAIRS[pair] + mi
-            if bh == 0:
-                grps[("h", m)] = hgp.tile([P, 2048], BF16, tag="hg", name="hg", align_bytes=64)
             hv = raws[("h", u)][:].rearrange("b t c -> b (t c)").bitcast(F32)
             hv = hv.rearrange("b (t m p u) -> b t m u p", t=2, m=2, u=2)
             tp = ps_b.tile([P, 2, 2, P], F32, tag="zp", name="tp")
             for t in range(2):
                 for w in range(2):
                     nc.tensor.transpose(tp[:, t, w, :], hv[:, t, mi, w, :], ident_f[:])
+            tps[(u, mi)] = tp
+
+        def h_evacuate(u, mi):
+            pair, bh = divmod(u, 2)
+            m = M_PAIRS[pair] + mi
+            if bh == 0:
+                grps[("h", m)] = hgp.tile([P, 2048], BF16, tag="hg", name="hg", align_bytes=64)
+            tp = tps[(u, mi)]
             dst = grps[("h", m)][:].bitcast(F32)[:, bh * 512:(bh + 1) * 512]
             nc.scalar.copy(
                 out=dst.rearrange("p (t b u) -> p t b u", t=2, u=2), in_=tp[:].rearrange("p t u b -> p t b u")
@@ -138,6 +146,11 @@ def tile_residualblock5_pb_t_kernel(tc, h, x, k2, b2, gamma2, beta2, mean2, var2
             nc.vector.quantize_mx(out=hw[:, m, :].bitcast(FP8X4), scales=hs[:, m, :], in_=grps[("h", m)][:])
             h_done.add(m)
 
+        jobs = [(n, 0, 512) for n in range(N_CHUNKS - TAPS)]
+        for c0 in (0, 256):
+            for n in range(N_CHUNKS - TAPS, N_CHUNKS):
+                jobs.append((n, c0, 256))
+        n_jobs = len(jobs)
         kws = {}
         kss = {}
         accs = {}
@@ -147,50 +160,56 @@ def tile_residualblock5_pb_t_kernel(tc, h, x, k2, b2, gamma2, beta2, mean2, var2
         pending = []
         bn_done = set()
 
-        def regroup(n):
-            g = grpp.tile([P, 2048], BF16, tag="grp", name="kgrp", align_bytes=64)
-            grps[("k", n)] = g
-            src = raws[("k", n)][:].rearrange("p (t c i) -> p c t i", t=4, i=4)
+        def regroup(n, c0, width):
+            g = grpp.tile([P, 4 * width], BF16, tag="grp", name="kgrp", align_bytes=64)
+            grps[("k", n, c0)] = g
+            src = raws[("k", n)][:].rearrange("p (t c i) -> p c t i", t=4, i=4)[:, c0 // 4:(c0 + width) // 4]
             dst = g[:].rearrange("p (c i t) -> p c t i", i=4, t=4)
-            cv = V_COLS // 4
+            cv = (V_TAIL if width < 512 else V_COLS) * width // 2048
             nc.vector.tensor_copy(out=dst[:, 0:cv], in_=src[:, 0:cv])
             nc.scalar.copy(out=dst[:, cv:], in_=src[:, cv:])
 
-        def quantise(n):
-            kws[n] = kwp.tile([P, 512], U32, tag="kw", name="kw", align_bytes=64)
-            kss[n] = kwp.tile([P, 512], U8, tag="ks", name="ks", align_bytes=64)
-            nc.vector.quantize_mx(out=kws[n][:].bitcast(FP8X4), scales=kss[n][:], in_=grps[("k", n)][:])
-            pending.append(n)
+        def quantise(n, c0, width):
+            kws[(n, c0)] = kwp.tile([P, width], U32, tag="kw", name="kw", align_bytes=64)
+            kss[(n, c0)] = kwp.tile([P, width], U8, tag="ks", name="ks", align_bytes=64)
+            nc.vector.quantize_mx(out=kws[(n, c0)][:].bitcast(FP8X4), scales=kss[(n, c0)][:], in_=grps[("k", n, c0)][:])
+            pending.append((n, c0, width))
+
+        def mx_pass(n, pair):
+            j, i = divmod(n, TAPS)
+            m = (ORDER[j] - STEP[taps_of(j)[i]]) % L
+            for ft in (2 * pair, 2 * pair + 1):
+                if i == 0:
+                    accs[(j, ft)] = ps_a.tile([P, 512], F32, tag="acc", name="acc")
+                c0 = 0 if (n, 0, 512) in jobs else 256 * pair
+                lo = ft * P - c0
+                nc.tensor.matmul_mx(
+                    out=accs[(j, ft)][:],
+                    lhsT=kws[(n, c0)][:, lo:lo + P].bitcast(FP8X4),
+                    lhsT_scale=kss[(n, c0)][:, lo:lo + P],
+                    rhs=hw[:, m, :].bitcast(FP8X4),
+                    rhs_scale=hs[:, m, :],
+                    start=(i == 0),
+                    stop=(i == TAPS - 1),
+                )
 
         def flush_mx():
             while len(pending) > 0:
-                n = pending[0]
+                n, c0, width = pending[0]
                 j, i = divmod(n, TAPS)
                 m = (ORDER[j] - STEP[taps_of(j)[i]]) % L
-                if i == 0 and j > 0 and (j - 1) not in bn_done:
-                    break
                 if m not in h_done:
                     break
                 pending.pop(0)
-                if i == 0:
-                    for ft in range(4):
-                        accs[(j, ft)] = ps_a.tile([P, 512], F32, tag="acc", name="acc")
-                for ft in range(4):
-                    nc.tensor.matmul_mx(
-                        out=accs[(j, ft)][:],
-                        lhsT=kws[n][:, ft * P:(ft + 1) * P].bitcast(FP8X4),
-                        lhsT_scale=kss[n][:, ft * P:(ft + 1) * P],
-                        rhs=hw[:, m, :].bitcast(FP8X4),
-                        rhs_scale=hs[:, m, :],
-                        start=(i == 0),
-                        stop=(i == TAPS - 1),
-                    )
+                mx_pass(n, c0 // 256)
+                if width == 512 and i == TAPS - 1:
+                    for q in range(TAPS):
+                        mx_pass(TAPS * j + q, 1)
 
-        def batch_norm(j):
-            bn_done.add(j)
-            for ft in range(4):
+        def batch_norm(j, pair, on_vector):
+            for ft in (2 * pair, 2 * pair + 1):
                 st = sp.tile([P, 512], F32, tag="s", name="s")
-                if j == L - 1 and ft % 2 == 1:
+                if ft in on_vector:
                     nc.vector.tensor_scalar(
                         out=st[:], in0=accs[(j, ft)][:], scalar1=a_sc[:, ft:ft + 1],
                         scalar2=b_sc[:, ORDER[j], ft:ft + 1], op0=ALU.mult, op1=ALU.add,
@@ -202,47 +221,57 @@ def tile_residualblock5_pb_t_kernel(tc, h, x, k2, b2, gamma2, beta2, mean2, var2
                     )
                 s_tiles[(j, ft)] = st
 
-        def add_x(j):
+        def back(j, pair):
             l0 = ORDER[j] // 2 * 2
-            for bt in range(4):
-                zp = ps_b.tile([P, 512], F32, tag="zp", name="zp")
-                zps[(j, bt)] = zp
-                lo = (ORDER[j] - l0) * 512
-                nc.tensor.matmul(
-                    out=zp[:], lhsT=ident_b[:], rhs=xs[l0][:, bt, lo:lo + 512], start=True, stop=False
-                )
-
-        def back(j):
-            for ft in range(4):
-                for bt in range(4):
-                    nc.tensor.matmul(
-                        out=zps[(j, bt)][:, ft * P:(ft + 1) * P],
-                        lhsT=s_tiles[(j, ft)][:, bt * P:(bt + 1) * P],
-                        rhs=ident_f[:],
-                        is_transpose=True,
-                        start=False,
-                        stop=(ft == 3),
-                    )
-
-        def copy_out(j, pair):
-            zs[(j, pair)] = zpool.tile([P, 2, 512], F32, tag="z", name="z")
+            lo = (ORDER[j] - l0) * 512 + 256 * pair
             for q in range(2):
-                nc.scalar.copy(out=zs[(j, pair)][:, q, :], in_=zps[(j, 2 * pair + q)][:])
+                zp = ps_b.tile([P, 2, 256], F32, tag="zp", name="zp")
+                zps[(j, pair, q)] = zp
+                nc.tensor.matmul(
+                    out=zp[:], lhsT=ident_b[:], rhs=xs[l0][:, 2 * q:2 * q + 2, lo:lo + 256], start=True, stop=False
+                )
+            for q in range(2):
+                for t in range(2):
+                    for f in range(2):
+                        bt = 2 * q + t
+                        nc.tensor.matmul(
+                            out=zps[(j, pair, q)][:, t, f * P:(f + 1) * P],
+                            lhsT=s_tiles[(j, 2 * pair + f)][:, bt * P:(bt + 1) * P],
+                            rhs=ident_f[:],
+                            is_transpose=True,
+                            start=False,
+                            stop=(t == 1 and f == 1),
+                        )
+
+        def copy_out(j, pair, qs, eng):
+            if (j, pair) not in zs:
+                if j == L - 1:
+                    zs[(j, pair)] = zpool.tile([P, 4, 256], F32, tag="z", name="z_half")[:]
+                else:
+                    if pair == 0:
+                        zs[j] = zpool.tile([P, 4, 512], F32, tag="z", name="z")
+                    zs[(j, pair)] = zs[j][:, :, 256 * pair:256 * pair + 256]
+            for q in qs:
+                dst = zs[(j, pair)][:, 2 * q:2 * q + 2, :]
+                if eng == "v":
+                    nc.vector.tensor_copy(out=dst, in_=zps[(j, pair, q)][:])
+                else:
+                    nc.scalar.copy(out=dst, in_=zps[(j, pair, q)][:])
 
         out_v = out.rearrange("(t p) l f -> p t l f", p=P)
 
+        def leaky(z):
+            nc.vector.scalar_tensor_tensor(out=z, in0=z, scalar=ALPHA, in1=z, op0=ALU.mult, op1=ALU.max)
+
         def leaky_store(j, pair):
-            z = zs[(j, pair)]
-            if j == L - 1:
-                for q in range(2):
-                    nc.vector.scalar_tensor_tensor(
-                        out=z[:, q, :], in0=z[:, q, :], scalar=ALPHA, in1=z[:, q, :], op0=ALU.mult, op1=ALU.max
-                    )
-                    nc.sync.dma_start(out=out_v[:, 2 * pair + q, ORDER[j], :], in_=z[:, q, :])
-            else:
-                zf = z[:].rearrange("p t f -> p (t f)")
-                nc.vector.scalar_tensor_tensor(out=zf, in0=zf, scalar=ALPHA, in1=zf, op0=ALU.mult, op1=ALU.max)
-                nc.sync.dma_start(out=out_v[:, 2 * pair:2 * pair + 2, ORDER[j], :], in_=z[:])
+            leaky(zs[(j, pair)])
+            if pair == 1:
+                nc.sync.dma_start(out=out_v[:, :, ORDER[j], :], in_=zs[j][:])
+
+        def leaky_store_half(j, pair, q):
+            z = zs[(j, pair)][:, 2 * q:2 * q + 2, :]
+            leaky(z)
+            nc.sync.dma_start(out=out_v[:, 2 * q:2 * q + 2, ORDER[j], 256 * pair:256 * pair + 256], in_=z)
 
         def bn_constants(k):
             if k == 0:
@@ -272,40 +301,65 @@ def tile_residualblock5_pb_t_kernel(tc, h, x, k2, b2, gamma2, beta2, mean2, var2
                     out=b_sc[:], in0=b_sc[:], in1=c_t[:, 4:8].unsqueeze(1).to_broadcast([P, L, 4]), op=ALU.add
                 )
 
-        h_evac = {0: [(0, 0), (0, 1)], 1: [(1, 0), (1, 1)], 2: [(2, 0), (2, 1)], 3: [(3, 0), (3, 1)],
-                  9: [(4, 0), (5, 0)], 10: [(4, 1), (5, 1)], 16: [(6, 0), (7, 0)], 21: [(6, 1), (7, 1)]}
-        h_quant = {2: [2, 3], 4: [1, 0], 10: [4], 11: [5], 17: [6], 22: [7]}
-        for n in range(N_CHUNKS + 8):
-            if n < N_CHUNKS:
-                regroup(n)
-                freed[0] += 1
+        h_tr = {0: [(0, 0), (0, 1)], 1: [(1, 0), (1, 1)], 2: [(2, 0), (2, 1)], 3: [(3, 0), (3, 1)],
+                7: [(4, 0), (5, 0)], 13: [(4, 1), (5, 1)], 18: [(6, 0), (7, 0)], 23: [(6, 1), (7, 1)]}
+        h_ev = {0: [(0, 0), (0, 1)], 1: [(1, 0), (1, 1)], 2: [(2, 0), (2, 1)], 3: [(3, 0), (3, 1)],
+                8: [(4, 0), (5, 0)], 14: [(4, 1), (5, 1)], 19: [(6, 0), (7, 0)], 24: [(6, 1), (7, 1)]}
+        h_quant = {2: [2, 3], 4: [1, 0], 9: [4], 15: [5], 20: [6], 25: [7]}
+        last = L - 1
+        qslot = []
+        for s in range(n_jobs):
+            if s < LAG2_FROM:
+                qslot.append(s + 1)
+            elif s < n_jobs - 1:
+                qslot.append(s + 2)
+            else:
+                qslot.append(s + 1)
+        for s in range(n_jobs + 12):
+            if s < n_jobs:
+                regroup(*jobs[s])
+                if s < N_CHUNKS - TAPS or s >= N_CHUNKS:
+                    freed[0] += 1
                 issue()
-            for u, mi in h_evac.get(n, []):
+            for u, mi in h_ev.get(s, []):
+                if u < 4:
+                    h_transpose(u, mi)
                 h_evacuate(u, mi)
-            for m in h_quant.get(n, []):
+            for m in h_quant.get(s, []):
                 h_quantise(m)
-            if 1 <= n < LAG_FROM:
-                quantise(n - 1)
-            elif LAG_FROM < n < N_CHUNKS:
-                quantise(n - 2)
-            elif n == N_CHUNKS:
-                quantise(n - 2)
-                quantise(n - 1)
-            bn_constants(n - 2)
-            for j in range(L):
-                e = TAPS * j + TAPS - 1 + (1 if LAG_FROM < TAPS * j + TAPS < N_CHUNKS else 0)
-                if n == e + 2:
-                    batch_norm(j)
-                    back(j)
-                if n == e + 4:
-                    copy_out(j, 0)
-                    copy_out(j, 1)
-                if n == e + 5:
+            for q in range(n_jobs):
+                if qslot[q] == s:
+                    quantise(*jobs[q])
+            bn_constants(s - 2)
+            for j in range(last):
+                e = TAPS * j + TAPS - 1
+                if s == e + 4:
+                    batch_norm(j, 0, ())
+                if s == e + 5:
+                    back(j, 0)
+                if s == e + 6:
+                    batch_norm(j, 1, ())
+                if s == e + 7:
+                    copy_out(j, 0, (0, 1), "s")
+                    back(j, 1)
+                if s == e + 8:
+                    copy_out(j, 1, (0, 1), "s")
+                if s == e + 9:
                     leaky_store(j, 0)
-                if n == e + 6:
+                if s == e + 10:
                     leaky_store(j, 1)
+            for u, mi in h_tr.get(s, []):
+                if u >= 4:
+                    h_transpose(u, mi)
+            for pair in range(2):
+                e = qslot[N_CHUNKS - TAPS + TAPS * pair + TAPS - 1] + (2 if pair == 0 else 0)
+                if s == e + 1:
+                    batch_norm(last, pair, () if pair == 0 else (3,))
+                    back(last, pair)
+                if s == e + 2:
+                    copy_out(last, pair, (0,), "s")
+                    copy_out(last, pair, (1,), "s" if pair == 0 else "v")
+                if s == e + 3:
+                    leaky_store_half(last, pair, 0)
+                    leaky_store_half(last, pair, 1)
             flush_mx()
-            for j in range(L):
-                e = TAPS * j + TAPS - 1 + (1 if LAG_FROM < TAPS * j + TAPS < N_CHUNKS else 0)
-                if n == e + 1:
-                    add_x(j)

@@ -21,7 +21,7 @@ BN_EPS = 1e-3
 ALPHA = 0.3
 N_CHUNKS = TAPS * L
 ORDER = (2, 3, 4, 5, 6, 7, 0, 1)
-RAW_BUFS = 10
+RAW_BUFS = 9
 V_COLS = 328
 V_TAIL = 416
 PIN = False
@@ -39,10 +39,10 @@ def tile_residualblock5_pb_t_kernel(tc, h, x, k2, b2, gamma2, beta2, mean2, var2
         const = ctx.enter_context(tc.tile_pool(name="const", bufs=1))
         rawp = ctx.enter_context(tc.tile_pool(name="rawp", bufs=RAW_BUFS))
         grpp = ctx.enter_context(tc.tile_pool(name="grpp", bufs=5))
-        kwp = ctx.enter_context(tc.tile_pool(name="kwp", bufs=10))
+        kwp = ctx.enter_context(tc.tile_pool(name="kwp", bufs=9))
         hgp = ctx.enter_context(tc.tile_pool(name="hgp", bufs=2))
         sp = ctx.enter_context(tc.tile_pool(name="sp", bufs=8))
-        zpool = ctx.enter_context(tc.tile_pool(name="zpool", bufs=3))
+        zpool = ctx.enter_context(tc.tile_pool(name="zpool", bufs=2))
         ps_a = ctx.enter_context(tc.psum_pool(name="ps_a", bufs=4))
         ps_b = ctx.enter_context(tc.psum_pool(name="ps_b", bufs=4))
         if PIN:
@@ -246,11 +246,15 @@ def tile_residualblock5_pb_t_kernel(tc, h, x, k2, b2, gamma2, beta2, mean2, var2
         def copy_out(j, pair, qs, eng):
             if (j, pair) not in zs:
                 if j == L - 1:
-                    zs[(j, pair)] = zpool.tile([P, 4, 256], F32, tag="z", name="z_half")[:]
-                else:
+                    zs[(j, pair)] = zpool.tile([P, 4, 256], F32, tag="zh", name="z_half")[:]
+                elif j == L - 2:
                     if pair == 0:
-                        zs[j] = zpool.tile([P, 4, 512], F32, tag="z", name="z")
+                        zs[j] = zpool.tile([P, 4, 512], F32, tag="zq", name="z_one", bufs=1)
                     zs[(j, pair)] = zs[j][:, :, 256 * pair:256 * pair + 256]
+                else:
+                    if pair == 0 and j % 2 == 0:
+                        zs[j // 2 * 2] = zpool.tile([P, 4, 2, 512], F32, tag="z", name="z")
+                    zs[(j, pair)] = zs[j // 2 * 2][:, :, j % 2, 256 * pair:256 * pair + 256]
             for q in qs:
                 dst = zs[(j, pair)][:, 2 * q:2 * q + 2, :]
                 if eng == "v":
@@ -265,8 +269,10 @@ def tile_residualblock5_pb_t_kernel(tc, h, x, k2, b2, gamma2, beta2, mean2, var2
 
         def leaky_store(j, pair):
             leaky(zs[(j, pair)])
-            if pair == 1:
+            if pair == 1 and j == L - 2:
                 nc.sync.dma_start(out=out_v[:, :, ORDER[j], :], in_=zs[j][:])
+            elif pair == 1 and j % 2 == 1:
+                nc.sync.dma_start(out=out_v[:, :, ORDER[j - 1]:ORDER[j] + 1, :], in_=zs[j - 1][:])
 
         def leaky_store_half(j, pair, q):
             z = zs[(j, pair)][:, 2 * q:2 * q + 2, :]

@@ -21,7 +21,7 @@ BN_EPS = 1e-3
 ALPHA = 0.3
 N_CHUNKS = TAPS * L
 ORDER = (2, 3, 4, 5, 6, 7, 0, 1)
-RAW_BUFS = 9
+RAW_BUFS = 13
 V_COLS = 328
 V_TAIL = 416
 PIN = False
@@ -40,6 +40,7 @@ def tile_residualblock5_pb_t_kernel(tc, h, x, k2, b2, gamma2, beta2, mean2, var2
         rawp = ctx.enter_context(tc.tile_pool(name="rawp", bufs=RAW_BUFS))
         grpp = ctx.enter_context(tc.tile_pool(name="grpp", bufs=5))
         kwp = ctx.enter_context(tc.tile_pool(name="kwp", bufs=9))
+        hrawp = ctx.enter_context(tc.tile_pool(name="hrawp", bufs=4))
         hgp = ctx.enter_context(tc.tile_pool(name="hgp", bufs=2))
         sp = ctx.enter_context(tc.tile_pool(name="sp", bufs=8))
         zpool = ctx.enter_context(tc.tile_pool(name="zpool", bufs=2))
@@ -73,7 +74,7 @@ def tile_residualblock5_pb_t_kernel(tc, h, x, k2, b2, gamma2, beta2, mean2, var2
                 if kind == "h":
                     pair, bh = divmod(idx, 2)
                     m0 = M_PAIRS[pair]
-                    ht = const.tile([P, 2, 1024], BF16, name="h_%d" % idx)
+                    ht = hrawp.tile([P, 2, 1024], BF16, tag="hraw", name="hraw")
                     nc.sync.dma_start(
                         out=ht[:],
                         in_=h.rearrange("(t p) l c -> p t (l c)", p=P)[:, 2 * bh:2 * bh + 2, m0 * 512:(m0 + 2) * 512],

from contextlib import ExitStack

import concourse.mybir as mybir
from concourse.masks import make_identity

FLOPS = 2 * 5 * 8 * 512 * 512 * 512

F32 = mybir.dt.float32
BF16 = mybir.dt.bfloat16
U32 = mybir.dt.uint32
U8 = mybir.dt.uint8
FP8X4 = mybir.dt.float8_e4m3fn_x4
ALU = mybir.AluOpType
ACT = mybir.ActivationFunctionType

P = 128
L = 8
TAPS = 5
STEP = (0, 0, 1, -1, 2)
BN_EPS = 1e-3
ALPHA = 0.3
N_CHUNKS = TAPS * L
ORDER = (2, 3, 4, 5, 6, 7, 0, 1)
RAW_BUFS = 13
V_COLS = 328
V_TAIL = 416
PIN = False
LOADS = (
    "k0 h0 k1 h1 k2 h2 k3 h3 k4 k5 h4 k6 h5 k7 k8 k9 x0 k10 k11 k12 k13 k14 k15 k16 k17 h6 k18 h7 k19 k20 x1 k21 k22 k23"
    " k24 k25 k26 k27 k28 k29 k30 x2 k31 k32 k33 k34 k35 k36 k37 k38 k39 x3"
)
M_PAIRS = (2, 0, 4, 6)
LAG2_FROM = 5


def tile_residualblock5_pb_t_kernel(tc, h, x, k2, b2, gamma2, beta2, mean2, var2, out):
    nc = tc.nc
    with ExitStack() as ctx:
        const = ctx.enter_context(tc.tile_pool(name="const", bufs=1))
        rawp = ctx.enter_context(tc.tile_pool(name="rawp", bufs=RAW_BUFS))
        grpp = ctx.enter_context(tc.tile_pool(name="grpp", bufs=5))
        kwp = ctx.enter_context(tc.tile_pool(name="kwp", bufs=9))
        hrawp = ctx.enter_context(tc.tile_pool(name="hrawp", bufs=4))
        hgp = ctx.enter_context(tc.tile_pool(name="hgp", bufs=2))
        sp = ctx.enter_context(tc.tile_pool(name="sp", bufs=8))
        zpool = ctx.enter_context(tc.tile_pool(name="zpool", bufs=2))
        ps_a = ctx.enter_context(tc.psum_pool(name="ps_a", bufs=4))
        ps_b = ctx.enter_context(tc.psum_pool(name="ps_b", bufs=4))
        if PIN:
            ctx.enter_context(tc.manual_schedule())

        loads = []
        for word in LOADS.split():
            loads.append((word[0], int(word[1:])))
        raws = {}
        xs = {}
        issued = [0, 0]

        def taps_of(j):
            return (0, 1, 3, 2, 4) if j == 0 else (0, 1, 2, 4, 3)

        def issue():
            while issued[0] < len(loads):
                kind, idx = loads[issued[0]]
                if kind == "x":
                    l0 = ORDER[2 * idx]
                    xt = const.tile([P, 4, 1024], BF16, name="x_%d" % idx)
                    nc.sync.dma_start(
                        out=xt[:], in_=x.rearrange("(t p) l f -> p t (l f)", p=P)[:, :, l0 * 512:(l0 + 2) * 512]
                    )
                    xs[l0] = xt
                    issued[0] += 1
                    continue
                if kind == "h":
                    pair, bh = divmod(idx, 2)
                    m0 = M_PAIRS[pair]
                    ht = hrawp.tile([P, 2, 1024], BF16, tag="hraw", name="hraw")
                    nc.sync.dma_start(
                        out=ht[:],
                        in_=h.rearrange("(t p) l c -> p t (l c)", p=P)[:, 2 * bh:2 * bh + 2, m0 * 512:(m0 + 2) * 512],
                    )
                    raws[("h", idx)] = ht
                    issued[0] += 1
                    continue
                if issued[1] >= RAW_BUFS + freed[0]:
                    return
                rt = rawp.tile([P, 2048], BF16, tag="raw", name="raw")
                j, i = divmod(idx, TAPS)
                nc.sync.dma_start(out=rt[:], in_=k2[taps_of(j)[i], ORDER[j]].rearrange("(p t) f -> p (t f)", t=4))
                raws[("k", idx)] = rt
                issued[0] += 1
                issued[1] += 1

        freed = [0]
        issue()

        ident_f = const.tile([P, P], F32, name="ident_f")
        make_identity(nc, ident_f[:])
        ident_b = const.tile([P, P], BF16, name="ident_b")
        warm = const.tile([P, 1], F32, name="warm")
        nc.vector.memset(warm[:], 1.0)
        cst = const.tile([P, P], BF16, name="cst")
        nc.vector.memset(cst[:], 0.0)
        nc.scalar.dma_start(out=cst[0:4, :], in_=gamma2.rearrange("(r c) -> r c", c=P))
        nc.scalar.dma_start(out=cst[4:8, :], in_=beta2.rearrange("(r c) -> r c", c=P))
        nc.scalar.dma_start(out=cst[8:12, :], in_=mean2.rearrange("(r c) -> r c", c=P))
        nc.scalar.dma_start(out=cst[12:16, :], in_=var2.rearrange("(r c) -> r c", c=P))
        nc.scalar.dma_start(out=cst[16:48, :], in_=b2.rearrange("l (r c) -> (l r) c", c=P))
        nc.scalar.activation(out=warm[:], in_=warm[:], func=ACT.Sqrt)
        nc.vector.tensor_copy(out=ident_b[:], in_=ident_f[:])
        c_t = const.tile([P, 48], F32, name="c_t")
        t_var = const.tile([P, 4], F32, name="t_var")
        t_std = const.tile([P, 4], F32, name="t_std")
        t_rstd = const.tile([P, 4], F32, name="t_rstd")
        a_sc = const.tile([P, 4], F32, name="a_sc")
        b_sc = const.tile([P, L, 4], F32, name="b_sc")
        hw = const.tile([P, L, 512], U32, name="hw", align_bytes=64)
        hs = const.tile([P, L, 512], U8, name="hs", align_bytes=64)

        grps = {}
        h_done = set()

        tps = {}

        def h_transpose(u, mi):
            pair, bh = divmod(u, 2)
            hv = raws[("h", u)][:].rearrange("b t c -> b (t c)").bitcast(F32)
            hv = hv.rearrange("b (t m p u) -> b t m u p", t=2, m=2, u=2)
            tp = ps_b.tile([P, 2, 2, P], F32, tag="zp", name="tp")
            for t in range(2):
                for w in range(2):
                    nc.tensor.transpose(tp[:, t, w, :], hv[:, t, mi, w, :], ident_f[:])
            tps[(u, mi)] = tp

        def h_evacuate(u, mi):
            pair, bh = divmod(u, 2)
            m = M_PAIRS[pair] + mi
            if bh == 0:
                grps[("h", m)] = hgp.tile([P, 2048], BF16, tag="hg", name="hg", align_bytes=64)
            tp = tps[(u, mi)]
            dst = grps[("h", m)][:].bitcast(F32)[:, bh * 512:(bh + 1) * 512]
            nc.scalar.copy(
                out=dst.rearrange("p (t b u) -> p t b u", t=2, u=2), in_=tp[:].rearrange("p t u b -> p t b u")
            )

        def h_quantise(m):
            nc.vector.quantize_mx(out=hw[:, m, :].bitcast(FP8X4), scales=hs[:, m, :], in_=grps[("h", m)][:])
            h_done.add(m)

        jobs = [(n, 0, 512) for n in range(N_CHUNKS - TAPS)]
        for c0 in (0, 256):
            for n in range(N_CHUNKS - TAPS, N_CHUNKS):
                jobs.append((n, c0, 256))
        n_jobs = len(jobs)
        kws = {}
        kss = {}
        accs = {}
        s_tiles = {}
        zps = {}
        zs = {}
        pending = []
        bn_done = set()

        def regroup(n, c0, width):
            g = grpp.tile([P, 4 * width], BF16, tag="grp", name="kgrp", align_bytes=64)
            grps[("k", n, c0)] = g
            src = raws[("k", n)][:].rearrange("p (t c i) -> p c t i", t=4, i=4)[:, c0 // 4:(c0 + width) // 4]
            dst = g[:].rearrange("p (c i t) -> p c t i", i=4, t=4)
            cv = (V_TAIL if width < 512 else V_COLS) * width // 2048
            nc.vector.tensor_copy(out=dst[:, 0:cv], in_=src[:, 0:cv])
            nc.scalar.copy(out=dst[:, cv:], in_=src[:, cv:])

        def quantise(n, c0, width):
            kws[(n, c0)] = kwp.tile([P, width], U32, tag="kw", name="kw", align_bytes=64)
            kss[(n, c0)] = kwp.tile([P, width], U8, tag="ks", name="ks", align_bytes=64)
            nc.vector.quantize_mx(out=kws[(n, c0)][:].bitcast(FP8X4), scales=kss[(n, c0)][:], in_=grps[("k", n, c0)][:])
            pending.append((n, c0, width))

        def mx_pass(n, pair):
            j, i = divmod(n, TAPS)
            m = (ORDER[j] - STEP[taps_of(j)[i]]) % L
            for ft in (2 * pair, 2 * pair + 1):
                if i == 0:
                    accs[(j, ft)] = ps_a.tile([P, 512], F32, tag="acc", name="acc")
                c0 = 0 if (n, 0, 512) in jobs else 256 * pair
                lo = ft * P - c0
                nc.tensor.matmul_mx(
                    out=accs[(j, ft)][:],
                    lhsT=kws[(n, c0)][:, lo:lo + P].bitcast(FP8X4),
                    lhsT_scale=kss[(n, c0)][:, lo:lo + P],
                    rhs=hw[:, m, :].bitcast(FP8X4),
                    rhs_scale=hs[:, m, :],
                    start=(i == 0),
                    stop=(i == TAPS - 1),
                )

        def flush_mx():
            while len(pending) > 0:
                n, c0, width = pending[0]
                j, i = divmod(n, TAPS)
                m = (ORDER[j] - STEP[taps_of(j)[i]]) % L
                if m not in h_done:
                    break
                pending.pop(0)
                mx_pass(n, c0 // 256)
                if width == 512 and i == TAPS - 1:
                    for q in range(TAPS):
                        mx_pass(TAPS * j + q, 1)

        def batch_norm(j, pair, on_vector):
            for ft in (2 * pair, 2 * pair + 1):
                st = sp.tile([P, 512], F32, tag="s", name="s")
                if ft in on_vector:
                    nc.vector.tensor_scalar(
                        out=st[:], in0=accs[(j, ft)][:], scalar1=a_sc[:, ft:ft + 1],
                        scalar2=b_sc[:, ORDER[j], ft:ft + 1], op0=ALU.mult, op1=ALU.add,
                    )
                else:
                    nc.scalar.activation(
                        out=st[:], in_=accs[(j, ft)][:], func=ACT.Identity,
                        scale=a_sc[:, ft:ft + 1], bias=b_sc[:, ORDER[j], ft:ft + 1],
                    )
                s_tiles[(j, ft)] = st

        def back(j, pair):
            l0 = ORDER[j] // 2 * 2
            lo = (ORDER[j] - l0) * 512 + 256 * pair
            for q in range(2):
                zp = ps_b.tile([P, 2, 256], F32, tag="zp", name="zp")
                zps[(j, pair, q)] = zp
                nc.tensor.matmul(
                    out=zp[:], lhsT=ident_b[:], rhs=xs[l0][:, 2 * q:2 * q + 2, lo:lo + 256], start=True, stop=False
                )
            for q in range(2):
                for t in range(2):
                    for f in range(2):
                        bt = 2 * q + t
                        nc.tensor.matmul(
                            out=zps[(j, pair, q)][:, t, f * P:(f + 1) * P],
                            lhsT=s_tiles[(j, 2 * pair + f)][:, bt * P:(bt + 1) * P],
                            rhs=ident_f[:],
                            is_transpose=True,
                            start=False,
                            stop=(t == 1 and f == 1),
                        )

        def copy_out(j, pair, qs, eng):
            if (j, pair) not in zs:
                if j == L - 1:
                    zs[(j, pair)] = zpool.tile([P, 4, 256], F32, tag="zh", name="z_half")[:]
                elif j == L - 2:
                    if pair == 0:
                        zs[j] = zpool.tile([P, 4, 512], F32, tag="zq", name="z_one", bufs=1)
                    zs[(j, pair)] = zs[j][:, :, 256 * pair:256 * pair + 256]
                else:
                    if pair == 0 and j % 2 == 0:
                        zs[j // 2 * 2] = zpool.tile([P, 4, 2, 512], F32, tag="z", name="z")
                    zs[(j, pair)] = zs[j // 2 * 2][:, :, j % 2, 256 * pair:256 * pair + 256]
            for q in qs:
                dst = zs[(j, pair)][:, 2 * q:2 * q + 2, :]
                if eng == "v":
                    nc.vector.tensor_copy(out=dst, in_=zps[(j, pair, q)][:])
                else:
                    nc.scalar.copy(out=dst, in_=zps[(j, pair, q)][:])

        out_v = out.rearrange("(t p) l f -> p t l f", p=P)

        def leaky(z):
            nc.vector.scalar_tensor_tensor(out=z, in0=z, scalar=ALPHA, in1=z, op0=ALU.mult, op1=ALU.max)

        def leaky_store(j, pair):
            leaky(zs[(j, pair)])
            if pair == 1 and j == L - 2:
                nc.sync.dma_start(out=out_v[:, :, ORDER[j], :], in_=zs[j][:])
            elif pair == 1 and j % 2 == 1:
                nc.sync.dma_start(out=out_v[:, :, ORDER[j - 1]:ORDER[j] + 1, :], in_=zs[j - 1][:])

        def leaky_store_half(j, pair, q):
            z = zs[(j, pair)][:, 2 * q:2 * q + 2, :]
            leaky(z)
            nc.sync.dma_start(out=out_v[:, 2 * q:2 * q + 2, ORDER[j], 256 * pair:256 * pair + 256], in_=z)

        def bn_constants(k):
            if k == 0:
                cps = ps_b.tile([P, P], BF16, tag="zp", name="cps")
                nc.tensor.transpose(cps[:], cst[:], ident_b[:])
                nc.vector.tensor_copy(out=c_t[:], in_=cps[:, 0:48])
                nc.vector.tensor_scalar(out=t_var[:], in0=c_t[:, 12:16], scalar1=BN_EPS, scalar2=None, op0=ALU.add)
            if k == 1:
                nc.scalar.activation(out=t_std[:], in_=t_var[:], func=ACT.Sqrt)
            if k == 2:
                nc.vector.reciprocal(out=t_rstd[:], in_=t_std[:])
                nc.vector.tensor_tensor(out=a_sc[:], in0=t_rstd[:], in1=c_t[:, 0:4], op=ALU.mult)
                nc.vector.scalar_tensor_tensor(
                    out=b_sc[:],
                    in0=c_t[:, 16:48].rearrange("p (l r) -> p l r", r=4),
                    scalar=2.0,
                    in1=c_t[:, 8:12].unsqueeze(1).to_broadcast([P, L, 4]),
                    op0=ALU.mult,
                    op1=ALU.subtract,
                )
            if k == 3:
                nc.vector.tensor_tensor(
                    out=b_sc[:], in0=b_sc[:], in1=a_sc[:].unsqueeze(1).to_broadcast([P, L, 4]), op=ALU.mult
                )
            if k == 4:
                nc.vector.tensor_tensor(
                    out=b_sc[:], in0=b_sc[:], in1=c_t[:, 4:8].unsqueeze(1).to_broadcast([P, L, 4]), op=ALU.add
                )

        h_tr = {0: [(0, 0), (0, 1)], 1: [(1, 0), (1, 1)], 2: [(2, 0), (2, 1)], 3: [(3, 0), (3, 1)],
                7: [(4, 0), (5, 0)], 13: [(4, 1), (5, 1)], 18: [(6, 0), (7, 0)], 23: [(6, 1), (7, 1)]}
        h_ev = {0: [(0, 0), (0, 1)], 1: [(1, 0), (1, 1)], 2: [(2, 0), (2, 1)], 3: [(3, 0), (3, 1)],
                8: [(4, 0), (5, 0)], 14: [(4, 1), (5, 1)], 19: [(6, 0), (7, 0)], 24: [(6, 1), (7, 1)]}
        h_quant = {2: [2, 3], 4: [1, 0], 9: [4], 15: [5], 20: [6], 25: [7]}
        last = L - 1
        qslot = []
        for s in range(n_jobs):
            if s < LAG2_FROM:
                qslot.append(s + 1)
            elif s < n_jobs - 1:
                qslot.append(s + 2)
            else:
                qslot.append(s + 1)
        for s in range(n_jobs + 12):
            if s < n_jobs:
                regroup(*jobs[s])
                if s < N_CHUNKS - TAPS or s >= N_CHUNKS:
                    freed[0] += 1
                issue()
            for u, mi in h_ev.get(s, []):
                if u < 4:
                    h_transpose(u, mi)
                h_evacuate(u, mi)
            for m in h_quant.get(s, []):
                h_quantise(m)
            for q in range(n_jobs):
                if qslot[q] == s:
                    quantise(*jobs[q])
            bn_constants(s - 2)
            for j in range(last):
                e = TAPS * j + TAPS - 1
                if s == e + 4:
                    batch_norm(j, 0, ())
                if s == e + 5:
                    back(j, 0)
                if s == e + 6:
                    batch_norm(j, 1, ())
                if s == e + 7:
                    copy_out(j, 0, (0, 1), "s")
                    back(j, 1)
                if s == e + 8:
                    copy_out(j, 1, (0, 1), "s")
                if s == e + 9:
                    leaky_store(j, 0)
                if s == e + 10:
                    leaky_store(j, 1)
            for u, mi in h_tr.get(s, []):
                if u >= 4:
                    h_transpose(u, mi)
            for pair in range(2):
                e = qslot[N_CHUNKS - TAPS + TAPS * pair + TAPS - 1] + (2 if pair == 0 else 0)
                if s == e + 1:
                    batch_norm(last, pair, () if pair == 0 else (3,))
                    back(last, pair)
                if s == e + 2:
                    copy_out(last, pair, (0,), "s")
                    copy_out(last, pair, (1,), "s" if pair == 0 else "v")
                if s == e + 3:
                    leaky_store_half(last, pair, 0)
                    leaky_store_half(last, pair, 1)
            flush_mx()
